import numpy as np
import ml_dtypes


def mxq(x, axis, fmt="e4m3"):
    dtype, down = {"e4m3": (ml_dtypes.float8_e4m3fn, 7), "e5m2": (ml_dtypes.float8_e5m2, 14)}[fmt]
    v = np.moveaxis(np.asarray(x, np.float32).astype(ml_dtypes.bfloat16).astype(np.float64), axis, -1)
    blocks = v.reshape(v.shape[:-1] + (-1, 32))
    amax = np.abs(blocks).max(-1, keepdims=True)
    byte = np.maximum(np.where(amax > 0, np.frexp(amax)[1] - 1 + 127, 0) - down, 1)
    scale = np.exp2(byte - 127.0)
    codes = (blocks / scale).astype(np.float32).astype(dtype).astype(np.float64)
    return np.moveaxis((codes * scale).reshape(v.shape), -1, axis)


WIDE = False


def mx_kscale(k):
    if not WIDE:
        return np.ones(k)
    levels = np.array([10, -10, 5, -5, 0])
    if k % 512:
        return np.exp2(np.random.permutation(np.resize(levels, k // 32))).repeat(32)
    a = np.empty((k // 512, 16))
    for p in range(k // 512):
        a[p, :8] = np.random.permutation(np.resize(levels, 8))
        for g in range(8):
            far = levels[np.abs(levels - a[p, g]) >= 10]
            a[p, g + 8] = far[np.random.randint(len(far))]
    return np.exp2(a.ravel()).repeat(32)


BF16 = ml_dtypes.bfloat16


def bf(x):
    return np.asarray(x, np.float32).astype(BF16)


def f64(x):
    return np.asarray(x).astype(np.float64)


S, B, H, NC, DC = 512, 16, 512, 8, 64
ROUTINGS = 4


def squash(x, axis=-1):
    s = np.sum(x * x, axis=axis, keepdims=True)
    return x / np.sqrt(s + 1e-7)


def softmax(v, axis):
    e = np.exp(v - v.max(axis=axis, keepdims=True))
    return e / e.sum(axis=axis, keepdims=True)


def setup_inputs():
    s = mx_kscale(H)
    std = np.sqrt(2.0 / (H + NC * DC))
    return {"inputs": bf(np.random.standard_normal((S, B, H)) * s),
            "W": bf(np.random.standard_normal((1, H, NC * DC)) * std / s[None, :, None])}


def reference(inputs, W):
    x = np.transpose(f64(inputs), (1, 0, 2))
    u = mxq(x, 2, "e4m3") @ mxq(f64(W)[0], 0, "e4m3")
    u = u.reshape(B, S, NC, DC)
    u = np.transpose(u, (0, 2, 1, 3))
    b = np.zeros((B, NC, S, 1))
    outputs = None
    for i in range(ROUTINGS):
        c = softmax(b, 1)
        outputs = squash(np.sum(c * u, axis=2))
        if i < ROUTINGS - 1:
            update = np.sum(outputs[:, :, None, :] * u, axis=-1, keepdims=True)
            b = b + update
    return outputs

@@ -1,0 +1,482 @@
+from contextlib import ExitStack
+
+import concourse.masks as masks
+import concourse.mybir as mybir
+
+F32 = mybir.dt.float32
+BF16 = mybir.dt.bfloat16
+U32 = mybir.dt.uint32
+U8 = mybir.dt.uint8
+FP8X4 = mybir.dt.float8_e4m3fn_x4
+ALU = mybir.AluOpType
+ACT = mybir.ActivationFunctionType
+AX = mybir.AxisListType
+
+S, B, H, NCAP, DC = 512, 16, 512, 8, 64
+ROUNDS = 4
+P = 128
+SJ = S // P
+DH = 4
+DL = DC // DH
+GB = 2
+NG = B // GB
+A = GB * SJ
+EPS = 1e-7
+NU = (ROUNDS - 1) * NG
+FINLAG = 23
+LEAD = 8
+PIN = True
+
+FLOPS = 2 * S * B * H * NCAP * DC + (2 * ROUNDS - 1) * 2 * S * B * NCAP * DC
+
+
+def gpsimd_dh(r):
+    return (2, 3)
+
+
+VECTOR_EVAC_DH = (1, 3)
+
+
+def tile_capsule_t_kernel(tc, inputs, W, out):
+    nc = tc.nc
+    with ExitStack() as ctx:
+        const = ctx.enter_context(tc.tile_pool(name="const", bufs=1))
+        xpool = ctx.enter_context(tc.tile_pool(name="xpool", bufs=2))
+        gpool = ctx.enter_context(tc.tile_pool(name="gpool", bufs=2))
+        qpool = ctx.enter_context(tc.tile_pool(name="qpool", bufs=2))
+        upool = ctx.enter_context(tc.tile_pool(name="upool", bufs=NG))
+        wpool = ctx.enter_context(tc.tile_pool(name="wpool", bufs=4))
+        cpool = ctx.enter_context(tc.tile_pool(name="cpool", bufs=3))
+        opool = ctx.enter_context(tc.tile_pool(name="opool", bufs=2))
+        small = ctx.enter_context(tc.tile_pool(name="small", bufs=NG + 1))
+        psum_n = ctx.enter_context(tc.psum_pool(name="psum_n", bufs=1))
+        psum_x = ctx.enter_context(tc.psum_pool(name="psum_x", bufs=4))
+        psum_y = ctx.enter_context(tc.psum_pool(name="psum_y", bufs=3))
+        if PIN:
+            ctx.enter_context(tc.manual_schedule())
+
+        ident = const.tile([P, P], F32, name="ident")
+        masks.make_identity(nc, ident[:])
+        m8 = const.tile([P, NCAP], F32, name="m8")
+        nc.vector.tensor_reduce(
+            out=m8[:], in_=ident[:].rearrange("p (n dl) -> p n dl", dl=DL), axis=AX.X, op=ALU.add
+        )
+        blk = const.tile([P, NCAP, DL], F32, name="blk")
+        nc.vector.tensor_copy(out=blk[:], in_=m8[:].unsqueeze(2).to_broadcast([P, NCAP, DL]))
+        neghalf = const.tile([P, GB], F32, name="neghalf")
+        nc.vector.memset(neghalf[:], -0.5)
+        zero = const.tile([P, 1], F32, name="zero")
+        nc.vector.memset(zero[:], 0.0)
+        epsc = const.tile([P, 1], F32, name="epsc")
+        nc.vector.memset(epsc[:], EPS)
+        ofin = const.tile([P, P], F32, name="ofin")
+        nc.vector.memset(ofin[:], 0.0)
+        junk = const.tile([P, S], F32, name="junk")
+        junk_s = const.tile([P, S], F32, name="junk_s")
+
+        xin = inputs.rearrange("(j p) b h -> p j b h", p=P)
+        st = {}
+        for q in range(NG):
+            st[q] = {}
+
+        def load(q):
+            x = xpool.tile([P, SJ, GB, H], BF16, name="x")
+            nc.sync.dma_start(out=x[:], in_=xin[:, :, q * GB : (q + 1) * GB, :])
+            st[q]["x32"] = x[:].bitcast(F32)
+
+        load(0)
+        wraw = const.tile([P, 4, NCAP * DC], BF16, name="wraw")
+        nc.sync.dma_start(
+            out=wraw[:],
+            in_=W[0].rearrange("(p t) c -> p t c", t=4),
+        )
+        load(1)
+        loaded = [2]
+
+        def load_up_to(n):
+            while loaded[0] < min(n, NG):
+                load(loaded[0])
+                loaded[0] += 1
+
+        wg = const.tile([P, DH, NCAP, DL, 4], BF16, name="wg", align_bytes=64)
+        wview = wraw[:].rearrange("p t (n dh dl) -> p dh n dl t", dh=DH, dl=DL)
+        for dh in range(DH):
+            nc.vector.tensor_copy(out=wg[:, dh], in_=wview[:, dh])
+        wq = const.tile([P, NCAP * DC], U32, name="wq", align_bytes=64)
+        ws = const.tile([P, NCAP * DC], U8, name="ws", align_bytes=64)
+        nc.vector.quantize_mx(
+            out=wq[:].bitcast(FP8X4),
+            scales=ws[:],
+            in_=wg[:].rearrange("p dh n dl t -> p (dh n dl t)"),
+        )
+
+        def st_t(q, bl):
+            s = st[q]
+            tiles = []
+            for half in range(2):
+                xt = psum_y.tile([P, 2, 2, P], F32, name="xt", tag="Y")
+                for jj in range(2):
+                    for uu in range(2):
+                        nc.tensor.transpose(
+                            xt[:, jj, uu, :],
+                            s["x32"][:, 2 * half + jj, bl, uu : 2 * P : 2],
+                            ident[:],
+                        )
+                tiles.append(xt)
+            s["xt", bl] = tiles
+
+        def st_xc(q, bl):
+            s = st[q]
+            grouped = gpool.tile([P, 4 * S], BF16, name="grouped", align_bytes=64)
+            g32 = grouped[:].bitcast(F32)
+            for half in range(2):
+                nc.scalar.copy(
+                    out=g32[:, 512 * half : 512 * half + 512].rearrange(
+                        "p (jj s uu) -> p jj s uu", jj=2, uu=2
+                    ),
+                    in_=s["xt", bl][half][:].rearrange("p jj uu s -> p jj s uu"),
+                )
+            s["grouped", bl] = grouped
+
+        def st_q(q, bl):
+            s = st[q]
+            xq = qpool.tile([P, S], U32, name="xq", align_bytes=64)
+            xs = qpool.tile([P, S], U8, name="xs", align_bytes=64)
+            nc.vector.quantize_mx(
+                out=xq[:].bitcast(FP8X4), scales=xs[:], in_=s["grouped", bl][:]
+            )
+            s["xq", bl] = (xq, xs)
+
+        def st_mev(q, bl):
+            s = st[q]
+            xq, xs = s["xq", bl]
+            if bl == 0:
+                s["u"] = upool.tile([P, GB, DH, S], F32, name="u")
+                s["v0s"] = small.tile([P, GB, DH], F32, name="v0s")
+                s["v"] = small.tile([P, GB, DH], F32, name="v")
+            for dh in range(DH):
+                pb = psum_x.tile([P, S], F32, name="pb", tag="X")
+                nc.tensor.matmul_mx(
+                    out=pb[:],
+                    lhsT=wq[:, P * dh : P * dh + P].bitcast(FP8X4),
+                    lhsT_scale=ws[:, P * dh : P * dh + P],
+                    rhs=xq[:].bitcast(FP8X4),
+                    rhs_scale=xs[:],
+                    start=True,
+                    stop=True,
+                )
+                s["pb", bl, dh] = pb
+                if dh in VECTOR_EVAC_DH:
+                    nc.vector.tensor_scalar(
+                        out=s["u"][:, bl, dh, :],
+                        in0=s["pb", bl, dh][:],
+                        scalar1=1.0,
+                        scalar2=None,
+                        op0=ALU.mult,
+                        op1=ALU.add,
+                        accum_out=s["v"][:, bl, dh : dh + 1],
+                    )
+                else:
+                    nc.scalar.activation(
+                        out=s["u"][:, bl, dh, :],
+                        in_=s["pb", bl, dh][:],
+                        func=ACT.Copy,
+                        accum_out=s["v0s"][:, bl, dh : dh + 1],
+                    )
+
+        def st_v0(q):
+            s = st[q]
+            nc.vector.tensor_copy(
+                out=s["v"][:].rearrange("p b (a e) -> p b a e", e=2)[:, :, :, 0],
+                in_=s["v0s"][:].rearrange("p b (a e) -> p b a e", e=2)[:, :, :, 0],
+            )
+
+        def st_a1(q, r):
+            s = st[q]
+            pre = 1.0 / NCAP if r == 0 else 1.0
+            sqj = small.tile([P, GB, DH], F32, name="sqj")
+            ssq = small.tile([P, GB], F32, name="ssq")
+            for bl in range(GB):
+                nc.scalar.activation(
+                    out=sqj[:, bl, :],
+                    in_=s["v"][:, bl, :],
+                    func=ACT.Square,
+                    scale=pre,
+                    accum_out=ssq[:, bl : bl + 1],
+                )
+            s["ssq"] = ssq
+
+        def st_a2(q):
+            s = st[q]
+            n_ps = psum_n.tile([P, GB], F32, name="n_ps", tag="n")
+            nc.tensor.matmul(
+                out=n_ps[:],
+                lhsT=blk[:].rearrange("p n dl -> p (n dl)"),
+                rhs=s["ssq"][:],
+                start=True,
+                stop=True,
+            )
+            s["n_ps"] = n_ps
+
+        def st_a3(q):
+            s = st[q]
+            xe = small.tile([P, GB], F32, name="xe")
+            nc.scalar.activation(
+                out=xe[:], in_=s["n_ps"][:], func=ACT.Identity, bias=epsc[:, 0:1]
+            )
+            s["xe"] = xe
+
+        def st_a4(q):
+            s = st[q]
+            rs = small.tile([P, GB], F32, name="rs")
+            nc.gpsimd.tensor_tensor(out=rs[:], in0=s["xe"][:], in1=neghalf[:], op=ALU.pow)
+            s["rs"] = rs
+
+        def st_a5(q, r):
+            s = st[q]
+            v = s["v"]
+            rsb = s["rs"][:].unsqueeze(2).to_broadcast([P, GB, DH])
+            if r == ROUNDS - 1:
+                nc.gpsimd.tensor_tensor(
+                    out=ofin[:, 0 : DH * B].rearrange("p (dh b) -> p b dh", dh=DH)[
+                        :, q * GB : (q + 1) * GB, :
+                    ],
+                    in0=v[:],
+                    in1=rsb,
+                    op=ALU.mult,
+                )
+                return
+            o = small.tile([P, GB, DH], F32, name="o")
+            nc.gpsimd.tensor_tensor(out=o[:], in0=v[:], in1=rsb, op=ALU.mult)
+            if r == 0:
+                ocum = small.tile([P, GB, DH], F32, name="ocum")
+                nc.gpsimd.tensor_scalar(
+                    out=ocum[:], in0=o[:], scalar1=1.0 / NCAP, scalar2=0.0, op0=ALU.mult, op1=ALU.add
+                )
+                s["ocum"] = ocum
+            else:
+                nc.gpsimd.tensor_tensor(out=s["ocum"][:], in0=s["ocum"][:], in1=o[:], op=ALU.add)
+
+        def st_b(q, r, bl):
+            s = st[q]
+            wt = wpool.tile([P, DH, S], F32, name="wt")
+            for dh in range(DH):
+                if dh in gpsimd_dh(r):
+                    nc.gpsimd.tensor_scalar(
+                        out=wt[:, dh, :],
+                        in0=s["u"][:, bl, dh, :],
+                        scalar1=s["ocum"][:, bl, dh : dh + 1],
+                        scalar2=zero[:, 0:1],
+                        op0=ALU.mult,
+                        op1=ALU.add,
+                    )
+                else:
+                    nc.scalar.activation(
+                        out=wt[:, dh, :],
+                        in_=s["u"][:, bl, dh, :],
+                        func=ACT.Copy,
+                        scale=s["ocum"][:, bl, dh : dh + 1],
+                    )
+            s["wt", bl] = wt
+
+        def st_c(q, bl):
+            s = st[q]
+            tp = psum_y.tile([P, SJ, P], F32, name="tp", tag="Y")
+            for j in range(SJ):
+                for dh in range(DH):
+                    nc.tensor.matmul(
+                        out=tp[:, j, :],
+                        lhsT=s["wt", bl][:, dh, P * j : P * j + P],
+                        rhs=ident[:],
+                        is_transpose=True,
+                        start=(dh == 0),
+                        stop=(dh == DH - 1),
+                    )
+            s["tp", bl] = tp
+
+        def st_d(q, bl):
+            s = st[q]
+            if bl == 0:
+                s["t"] = small.tile([P, A, NCAP], F32, name="t")
+            nc.vector.tensor_reduce(
+                out=s["t"][:, bl * SJ : (bl + 1) * SJ, :],
+                in_=s["tp", bl][:].rearrange("p j (n dl) -> p j n dl", dl=DL),
+                axis=AX.X,
+                op=ALU.add,
+            )
+
+        def st_e1(q):
+            s = st[q]
+            nmx = small.tile([P, A], F32, name="nmx")
+            nc.vector.tensor_reduce(
+                out=nmx[:], in_=s["t"][:], axis=AX.X, op=ALU.max, negate=True
+            )
+            s["nmx"] = nmx
+
+        def st_e2(q):
+            s = st[q]
+            ex = small.tile([P, A, NCAP], F32, name="ex")
+            sm = small.tile([P, A], F32, name="sm")
+            for a in range(A):
+                nc.scalar.activation(
+                    out=ex[:, a, :],
+                    in_=s["t"][:, a, :],
+                    func=ACT.Exp,
+                    bias=s["nmx"][:, a : a + 1],
+                    accum_out=sm[:, a : a + 1],
+                )
+            s["ex"] = ex
+            s["sm"] = sm
+
+        def st_e3(q):
+            s = st[q]
+            rc = small.tile([P, A], F32, name="rc")
+            nc.vector.reciprocal(out=rc[:], in_=s["sm"][:])
+            s["rc"] = rc
+
+        def st_e4(q, bl):
+            s = st[q]
+            crep = cpool.tile([P, SJ, NCAP, DL], F32, name="crep")
+            for j in range(SJ):
+                a = bl * SJ + j
+                nc.scalar.activation(
+                    out=crep[:, j],
+                    in_=s["ex"][:, a, :].unsqueeze(2).to_broadcast([P, NCAP, DL]),
+                    func=ACT.Copy,
+                    scale=s["rc"][:, a : a + 1],
+                )
+            s["crep", bl] = crep
+
+        def st_f(q, bl):
+            s = st[q]
+            cb = psum_x.tile([P, SJ, P], F32, name="cb", tag="X")
+            for j in range(SJ):
+                nc.tensor.transpose(
+                    cb[:, j, :], s["crep", bl][:, j].rearrange("p n dl -> p (n dl)"), ident[:]
+                )
+            s["cb", bl] = cb
+
+        def st_g(q, bl):
+            s = st[q]
+            if bl == 0:
+                s["vv"] = small.tile([P, GB, DH], F32, name="vv")
+            for dh in range(DH - bl):
+                nc.vector.scalar_tensor_tensor(
+                    out=junk[:],
+                    in0=s["u"][:, bl, dh, :],
+                    scalar=1.0,
+                    in1=s["cb", bl][:].rearrange("p j s -> p (j s)"),
+                    op0=ALU.mult,
+                    op1=ALU.mult,
+                    accum_out=s["vv"][:, bl, dh : dh + 1],
+                )
+
+        def st_go12(q):
+            s = st[q]
+            cbs = opool.tile([P, S], F32, name="cbs")
+            nc.scalar.copy(out=cbs[:], in_=s["cb", 1][:].rearrange("p j s -> p (j s)"))
+            prod = opool.tile([P, S], F32, name="prod")
+            nc.gpsimd.tensor_tensor(out=prod[:], in0=s["u"][:, 1, 3, :], in1=cbs[:], op=ALU.mult)
+            s["prod"] = prod
+
+        def st_go3(q):
+            s = st[q]
+            v = small.tile([P, GB, DH], F32, name="v")
+            nc.scalar.activation(
+                out=junk_s[:], in_=s["prod"][:], func=ACT.Copy, accum_out=v[:, 1, 3:4]
+            )
+            nc.scalar.copy(out=v[:, 0, :], in_=s["vv"][:, 0, :])
+            nc.scalar.copy(out=v[:, 1, 0:3], in_=s["vv"][:, 1, 0:3])
+            s["v"] = v
+
+        def unit(k):
+            return (k // NG, k % NG)
+
+        def is_unit(k):
+            return 0 <= k < NU
+
+        def squashes(k):
+            found = []
+            if is_unit(k):
+                found.append(unit(k))
+            if 0 <= k - 1 - FINLAG < NG:
+                found.append((ROUNDS - 1, k - 1 - FINLAG))
+            return found
+
+        def is_batch(b):
+            return 0 <= b < B
+
+        step = [-2]
+
+        def proj_step():
+            b = step[0]
+            step[0] += 1
+            if is_batch(b + 2) and (b + 2) % GB == 0:
+                load_up_to((b + 2) // GB + 2)
+            if is_batch(b + 1):
+                st_q((b + 1) // GB, (b + 1) % GB)
+            if is_batch(b):
+                st_mev(b // GB, b % GB)
+                if b % GB == GB - 1:
+                    st_v0(b // GB)
+            if is_batch(b + 2):
+                st_t((b + 2) // GB, (b + 2) % GB)
+                st_xc((b + 2) // GB, (b + 2) % GB)
+
+        while step[0] < LEAD:
+            proj_step()
+
+        for t in range(-2, FINLAG + NG + 2):
+            for r, q in squashes(t + 2):
+                st_a1(q, r)
+            if is_unit(t):
+                r, q = unit(t)
+                st_b(q, r, 0)
+                st_b(q, r, 1)
+            if is_unit(t - 4):
+                st_go12(unit(t - 4)[1])
+            if is_unit(t - 2):
+                q = unit(t - 2)[1]
+                st_d(q, 0)
+                st_d(q, 1)
+            for r, q in squashes(t + 1):
+                st_a3(q)
+                st_a4(q)
+            proj_step()
+            if is_unit(t - 1):
+                q = unit(t - 1)[1]
+                st_c(q, 0)
+                st_c(q, 1)
+            if is_unit(t - 3):
+                q = unit(t - 3)[1]
+                st_f(q, 0)
+                st_f(q, 1)
+            if is_unit(t - 4):
+                st_g(unit(t - 4)[1], 0)
+            if is_unit(t - 2):
+                q = unit(t - 2)[1]
+                st_e1(q)
+                st_e2(q)
+            proj_step()
+            if is_unit(t - 4):
+                st_g(unit(t - 4)[1], 1)
+            if is_unit(t - 2):
+                q = unit(t - 2)[1]
+                st_e3(q)
+                st_e4(q, 0)
+                st_e4(q, 1)
+            if is_unit(t - 4):
+                st_go3(unit(t - 4)[1])
+            for r, q in squashes(t + 1):
+                st_a5(q, r)
+            for r, q in squashes(t + 2):
+                st_a2(q)
+
+        of_ps = psum_y.tile([P, P], F32, name="of_ps", tag="Y")
+        nc.tensor.transpose(of_ps[:], ofin[:], ident[:])
+        of_sb = const.tile([P, NCAP, DL], F32, name="of_sb")
+        nc.vector.tensor_copy(out=of_sb[:].rearrange("p n dl -> p (n dl)"), in_=of_ps[:])
+        for dh in range(DH):
+            nc.sync.dma_start(
+                out=out[:, :, DL * dh : DL * dh + DL], in_=of_sb[B * dh : B * dh + B, :, :]
+            )

@@ -23,18 +23,24 @@ NG = B // GB
 A = GB * SJ
 EPS = 1e-7
 NU = (ROUNDS - 1) * NG
-FINLAG = 23
+SQUASH_LAG = 6
 LEAD = 8
 PIN = True
+
+
+def gpsimd_scales(k, i):
+    return i not in (0, 1, 4)
+
+
+def gpsimd_sums(k):
+    return 1
+
 
 FLOPS = 2 * S * B * H * NCAP * DC + (2 * ROUNDS - 1) * 2 * S * B * NCAP * DC
 
 
-def gpsimd_dh(r):
-    return (2, 3)
-
-
-VECTOR_EVAC_DH = (1, 3)
+def vector_evac_dh(b):
+    return (1, 3)
 
 
 def tile_capsule_t_kernel(tc, inputs, W, out):
@@ -63,10 +69,8 @@ def tile_capsule_t_kernel(tc, inputs, W, out):
         )
         blk = const.tile([P, NCAP, DL], F32, name="blk")
         nc.vector.tensor_copy(out=blk[:], in_=m8[:].unsqueeze(2).to_broadcast([P, NCAP, DL]))
-        neghalf = const.tile([P, GB], F32, name="neghalf")
+        neghalf = const.tile([P, 2 * GB], F32, name="neghalf")
         nc.vector.memset(neghalf[:], -0.5)
-        zero = const.tile([P, 1], F32, name="zero")
-        nc.vector.memset(zero[:], 0.0)
         epsc = const.tile([P, 1], F32, name="epsc")
         nc.vector.memset(epsc[:], EPS)
         ofin = const.tile([P, P], F32, name="ofin")
@@ -152,7 +156,6 @@ def tile_capsule_t_kernel(tc, inputs, W, out):
             xq, xs = s["xq", bl]
             if bl == 0:
                 s["u"] = upool.tile([P, GB, DH, S], F32, name="u")
-                s["v0s"] = small.tile([P, GB, DH], F32, name="v0s")
                 s["v"] = small.tile([P, GB, DH], F32, name="v")
             for dh in range(DH):
                 pb = psum_x.tile([P, S], F32, name="pb", tag="X")
@@ -166,7 +169,7 @@ def tile_capsule_t_kernel(tc, inputs, W, out):
                     stop=True,
                 )
                 s["pb", bl, dh] = pb
-                if dh in VECTOR_EVAC_DH:
+                if dh in vector_evac_dh(q * GB + bl):
                     nc.vector.tensor_scalar(
                         out=s["u"][:, bl, dh, :],
                         in0=s["pb", bl, dh][:],
@@ -181,92 +184,78 @@ def tile_capsule_t_kernel(tc, inputs, W, out):
                         out=s["u"][:, bl, dh, :],
                         in_=s["pb", bl, dh][:],
                         func=ACT.Copy,
-                        accum_out=s["v0s"][:, bl, dh : dh + 1],
+                        accum_out=s["v"][:, bl, dh : dh + 1],
                     )
 
-        def st_v0(q):
-            s = st[q]
-            nc.vector.tensor_copy(
-                out=s["v"][:].rearrange("p b (a e) -> p b a e", e=2)[:, :, :, 0],
-                in_=s["v0s"][:].rearrange("p b (a e) -> p b a e", e=2)[:, :, :, 0],
-            )
-
-        def st_a1(q, r):
-            s = st[q]
+        def st_a1(qs, r):
             pre = 1.0 / NCAP if r == 0 else 1.0
-            sqj = small.tile([P, GB, DH], F32, name="sqj")
-            ssq = small.tile([P, GB], F32, name="ssq")
-            for bl in range(GB):
-                nc.scalar.activation(
-                    out=sqj[:, bl, :],
-                    in_=s["v"][:, bl, :],
-                    func=ACT.Square,
-                    scale=pre,
-                    accum_out=ssq[:, bl : bl + 1],
-                )
-            s["ssq"] = ssq
+            sqj = small.tile([P, DH], F32, name="sqj")
+            ssq = small.tile([P, 2 * GB], F32, name="ssq")
+            for i, q in enumerate(qs):
+                for bl in range(GB):
+                    nc.scalar.activation(
+                        out=sqj[:],
+                        in_=st[q]["v"][:, bl, :],
+                        func=ACT.Square,
+                        scale=pre,
+                        accum_out=ssq[:, i * GB + bl : i * GB + bl + 1],
+                    )
+            return ssq
 
-        def st_a2(q):
-            s = st[q]
-            n_ps = psum_n.tile([P, GB], F32, name="n_ps", tag="n")
+        def st_a2(qs, ssq):
+            n = len(qs) * GB
+            n_ps = psum_n.tile([P, 2 * GB], F32, name="n_ps", tag="n")
             nc.tensor.matmul(
-                out=n_ps[:],
+                out=n_ps[:, 0:n],
                 lhsT=blk[:].rearrange("p n dl -> p (n dl)"),
-                rhs=s["ssq"][:],
+                rhs=ssq[:, 0:n],
                 start=True,
                 stop=True,
             )
-            s["n_ps"] = n_ps
-
-        def st_a3(q):
-            s = st[q]
-            xe = small.tile([P, GB], F32, name="xe")
+            xe = small.tile([P, 2 * GB], F32, name="xe")
             nc.scalar.activation(
-                out=xe[:], in_=s["n_ps"][:], func=ACT.Identity, bias=epsc[:, 0:1]
+                out=xe[:, 0:n], in_=n_ps[:, 0:n], func=ACT.Identity, bias=epsc[:, 0:1]
             )
-            s["xe"] = xe
+            return xe
 
-        def st_a4(q):
-            s = st[q]
-            rs = small.tile([P, GB], F32, name="rs")
-            nc.gpsimd.tensor_tensor(out=rs[:], in0=s["xe"][:], in1=neghalf[:], op=ALU.pow)
-            s["rs"] = rs
+        def st_a4(qs, r, xe):
+            n = len(qs) * GB
+            rs = small.tile([P, 2 * GB], F32, name="rs")
+            nc.gpsimd.tensor_tensor(out=rs[:, 0:n], in0=xe[:, 0:n], in1=neghalf[:, 0:n], op=ALU.pow)
+            for i, q in enumerate(qs):
+                s = st[q]
+                rsb = rs[:, i * GB : (i + 1) * GB].unsqueeze(2).to_broadcast([P, GB, DH])
+                if r == ROUNDS - 1:
+                    nc.gpsimd.tensor_tensor(
+                        out=ofin[:, 0 : DH * B].rearrange("p (dh b) -> p b dh", dh=DH)[
+                            :, q * GB : (q + 1) * GB, :
+                        ],
+                        in0=s["v"][:],
+                        in1=rsb,
+                        op=ALU.mult,
+                    )
+                    continue
+                o = small.tile([P, GB, DH], F32, name="o")
+                nc.gpsimd.tensor_tensor(out=o[:], in0=s["v"][:], in1=rsb, op=ALU.mult)
+                if r == 0:
+                    ocum = small.tile([P, GB, DH], F32, name="ocum")
+                    nc.gpsimd.tensor_scalar(
+                        out=ocum[:], in0=o[:], scalar1=1.0 / NCAP, scalar2=0.0, op0=ALU.mult, op1=ALU.add
+                    )
+                    s["ocum"] = ocum
+                else:
+                    nc.gpsimd.tensor_tensor(out=s["ocum"][:], in0=s["ocum"][:], in1=o[:], op=ALU.add)
 
-        def st_a5(q, r):
-            s = st[q]
-            v = s["v"]
-            rsb = s["rs"][:].unsqueeze(2).to_broadcast([P, GB, DH])
-            if r == ROUNDS - 1:
-                nc.gpsimd.tensor_tensor(
-                    out=ofin[:, 0 : DH * B].rearrange("p (dh b) -> p b dh", dh=DH)[
-                        :, q * GB : (q + 1) * GB, :
-                    ],
-                    in0=v[:],
-                    in1=rsb,
-                    op=ALU.mult,
-                )
-                return
-            o = small.tile([P, GB, DH], F32, name="o")
-            nc.gpsimd.tensor_tensor(out=o[:], in0=v[:], in1=rsb, op=ALU.mult)
-            if r == 0:
-                ocum = small.tile([P, GB, DH], F32, name="ocum")
-                nc.gpsimd.tensor_scalar(
-                    out=ocum[:], in0=o[:], scalar1=1.0 / NCAP, scalar2=0.0, op0=ALU.mult, op1=ALU.add
-                )
-                s["ocum"] = ocum
-            else:
-                nc.gpsimd.tensor_tensor(out=s["ocum"][:], in0=s["ocum"][:], in1=o[:], op=ALU.add)
-
-        def st_b(q, r, bl):
-            s = st[q]
+        def st_b(k, bl):
+            s = st[k % NG]
             wt = wpool.tile([P, DH, S], F32, name="wt")
             for dh in range(DH):
-                if dh in gpsimd_dh(r):
+                if gpsimd_scales(k, bl * DH + dh):
                     nc.gpsimd.tensor_scalar(
                         out=wt[:, dh, :],
                         in0=s["u"][:, bl, dh, :],
                         scalar1=s["ocum"][:, bl, dh : dh + 1],
-                        scalar2=zero[:, 0:1],
+                        scalar2=0.0,
                         op0=ALU.mult,
                         op1=ALU.add,
                     )
@@ -307,44 +296,60 @@ def tile_capsule_t_kernel(tc, inputs, W, out):
 
         def st_e1(q):
             s = st[q]
-            nmx = small.tile([P, A], F32, name="nmx")
-            nc.vector.tensor_reduce(
-                out=nmx[:], in_=s["t"][:], axis=AX.X, op=ALU.max, negate=True
-            )
-            s["nmx"] = nmx
+            mx = small.tile([P, A], F32, name="mx")
+            nc.vector.tensor_reduce(out=mx[:], in_=s["t"][:], axis=AX.X, op=ALU.max)
+            s["mx"] = mx
 
         def st_e2(q):
             s = st[q]
-            ex = small.tile([P, A, NCAP], F32, name="ex")
-            sm = small.tile([P, A], F32, name="sm")
-            for a in range(A):
-                nc.scalar.activation(
-                    out=ex[:, a, :],
-                    in_=s["t"][:, a, :],
-                    func=ACT.Exp,
-                    bias=s["nmx"][:, a : a + 1],
-                    accum_out=sm[:, a : a + 1],
-                )
-            s["ex"] = ex
-            s["sm"] = sm
+            td = small.tile([P, A, NCAP], F32, name="td")
+            nc.vector.tensor_tensor(
+                out=td[:],
+                in0=s["t"][:],
+                in1=s["mx"][:].unsqueeze(2).to_broadcast([P, A, NCAP]),
+                op=ALU.subtract,
+            )
+            s["td"] = td
 
         def st_e3(q):
+            s = st[q]
+            ex = small.tile([P, A, NCAP], F32, name="ex")
+            nc.scalar.activation(out=ex[:], in_=s["td"][:], func=ACT.Exp)
+            s["ex"] = ex
+
+        def st_e4(q):
+            s = st[q]
+            sm = small.tile([P, A], F32, name="sm")
+            nc.vector.tensor_reduce(out=sm[:], in_=s["ex"][:], axis=AX.X, op=ALU.add)
+            s["sm"] = sm
+
+        def st_e5(q):
             s = st[q]
             rc = small.tile([P, A], F32, name="rc")
             nc.vector.reciprocal(out=rc[:], in_=s["sm"][:])
             s["rc"] = rc
 
-        def st_e4(q, bl):
+        def st_e6(q):
             s = st[q]
-            crep = cpool.tile([P, SJ, NCAP, DL], F32, name="crep")
-            for j in range(SJ):
-                a = bl * SJ + j
-                nc.scalar.activation(
-                    out=crep[:, j],
-                    in_=s["ex"][:, a, :].unsqueeze(2).to_broadcast([P, NCAP, DL]),
-                    func=ACT.Copy,
-                    scale=s["rc"][:, a : a + 1],
-                )
+            c = small.tile([P, A, NCAP], F32, name="c")
+            nc.vector.tensor_tensor(
+                out=c[:],
+                in0=s["ex"][:],
+                in1=s["rc"][:].unsqueeze(2).to_broadcast([P, A, NCAP]),
+                op=ALU.mult,
+            )
+            s["c"] = c
+
+        def st_e7(q, bl):
+            s = st[q]
+            crep = cpool.tile([P, SJ * NCAP, DL], F32, name="crep")
+            nc.scalar.copy(
+                out=crep[:],
+                in_=s["c"][:, bl * SJ : (bl + 1) * SJ, :]
+                .rearrange("p j n -> p (j n)")
+                .unsqueeze(2)
+                .to_broadcast([P, SJ * NCAP, DL]),
+            )
             s["crep", bl] = crep
 
         def st_f(q, bl):
@@ -352,42 +357,53 @@ def tile_capsule_t_kernel(tc, inputs, W, out):
             cb = psum_x.tile([P, SJ, P], F32, name="cb", tag="X")
             for j in range(SJ):
                 nc.tensor.transpose(
-                    cb[:, j, :], s["crep", bl][:, j].rearrange("p n dl -> p (n dl)"), ident[:]
+                    cb[:, j, :],
+                    s["crep", bl][:, j * NCAP : (j + 1) * NCAP, :].rearrange("p n dl -> p (n dl)"),
+                    ident[:],
                 )
             s["cb", bl] = cb
 
-        def st_g(q, bl):
-            s = st[q]
-            if bl == 0:
-                s["vv"] = small.tile([P, GB, DH], F32, name="vv")
-            for dh in range(DH - bl):
-                nc.vector.scalar_tensor_tensor(
-                    out=junk[:],
-                    in0=s["u"][:, bl, dh, :],
-                    scalar=1.0,
-                    in1=s["cb", bl][:].rearrange("p j s -> p (j s)"),
-                    op0=ALU.mult,
-                    op1=ALU.mult,
-                    accum_out=s["vv"][:, bl, dh : dh + 1],
-                )
+        def st_g(k, i):
+            s = st[k % NG]
+            if i == 0:
+                s["v"] = small.tile([P, GB, DH], F32, name="v")
+            nc.vector.scalar_tensor_tensor(
+                out=junk[:],
+                in0=s["u"][:, i // DH, i % DH, :],
+                scalar=1.0,
+                in1=s["cb", i // DH][:].rearrange("p j s -> p (j s)"),
+                op0=ALU.mult,
+                op1=ALU.mult,
+                accum_out=s["v"][:, i // DH, i % DH : i % DH + 1],
+            )
 
-        def st_go12(q):
-            s = st[q]
+        def st_go1(k):
+            n = gpsimd_sums(k)
+            if n == 0:
+                return
+            s = st[k % NG]
             cbs = opool.tile([P, S], F32, name="cbs")
             nc.scalar.copy(out=cbs[:], in_=s["cb", 1][:].rearrange("p j s -> p (j s)"))
-            prod = opool.tile([P, S], F32, name="prod")
-            nc.gpsimd.tensor_tensor(out=prod[:], in0=s["u"][:, 1, 3, :], in1=cbs[:], op=ALU.mult)
+            prod = opool.tile([P, n, S], F32, name="prod")
+            nc.gpsimd.tensor_tensor(
+                out=prod[:],
+                in0=s["u"][:, 1, DH - n :, :],
+                in1=cbs[:].unsqueeze(1).to_broadcast([P, n, S]),
+                op=ALU.mult,
+            )
             s["prod"] = prod
 
-        def st_go3(q):
-            s = st[q]
-            v = small.tile([P, GB, DH], F32, name="v")
-            nc.scalar.activation(
-                out=junk_s[:], in_=s["prod"][:], func=ACT.Copy, accum_out=v[:, 1, 3:4]
-            )
-            nc.scalar.copy(out=v[:, 0, :], in_=s["vv"][:, 0, :])
-            nc.scalar.copy(out=v[:, 1, 0:3], in_=s["vv"][:, 1, 0:3])
-            s["v"] = v
+        def st_go3(k):
+            n = gpsimd_sums(k)
+            s = st[k % NG]
+            for i in range(n):
+                dh = DH - n + i
+                nc.scalar.activation(
+                    out=junk_s[:],
+                    in_=s["prod"][:, i, :],
+                    func=ACT.Copy,
+                    accum_out=s["v"][:, 1, dh : dh + 1],
+                )
 
         def unit(k):
             return (k // NG, k % NG)
@@ -395,13 +411,16 @@ def tile_capsule_t_kernel(tc, inputs, W, out):
         def is_unit(k):
             return 0 <= k < NU
 
-        def squashes(k):
-            found = []
-            if is_unit(k):
-                found.append(unit(k))
-            if 0 <= k - 1 - FINLAG < NG:
-                found.append((ROUNDS - 1, k - 1 - FINLAG))
-            return found
+        def squash_of(t):
+            k = t + 2
+            if 0 <= k < NG:
+                return ([k], 0)
+            if NG <= k < NU and k % 2 == 0:
+                return ([k % NG, k % NG + 1], k // NG)
+            q = t - (NU - NG) - SQUASH_LAG
+            if 0 <= q < NG and q % 2 == 0:
+                return ([q, q + 1], ROUNDS - 1)
+            return None
 
         def is_batch(b):
             return 0 <= b < B
@@ -417,8 +436,6 @@ def tile_capsule_t_kernel(tc, inputs, W, out):
                 st_q((b + 1) // GB, (b + 1) % GB)
             if is_batch(b):
                 st_mev(b // GB, b % GB)
-                if b % GB == GB - 1:
-                    st_v0(b // GB)
             if is_batch(b + 2):
                 st_t((b + 2) // GB, (b + 2) % GB)
                 st_xc((b + 2) // GB, (b + 2) % GB)
@@ -426,51 +443,63 @@ def tile_capsule_t_kernel(tc, inputs, W, out):
         while step[0] < LEAD:
             proj_step()
 
-        for t in range(-2, FINLAG + NG + 2):
-            for r, q in squashes(t + 2):
-                st_a1(q, r)
+        xe = {}
+        for t in range(-2, NU + SQUASH_LAG):
+            g = t - 4 if is_unit(t - 4) else None
+            e = (t - 2) % NG if is_unit(t - 2) else None
+            sq = squash_of(t)
+            sq1 = squash_of(t - 1)
+
+            def weigh(*todo):
+                if g is not None:
+                    for i in todo:
+                        if i < GB * DH - gpsimd_sums(g):
+                            st_g(g, i)
+
+            if sq:
+                ssq = st_a1(*sq)
+            if g is not None:
+                st_go1(g)
+            if e is not None:
+                st_d(e, 0)
+                st_d(e, 1)
+            weigh(0)
+            if e is not None:
+                st_e1(e)
             if is_unit(t):
-                r, q = unit(t)
-                st_b(q, r, 0)
-                st_b(q, r, 1)
-            if is_unit(t - 4):
-                st_go12(unit(t - 4)[1])
-            if is_unit(t - 2):
-                q = unit(t - 2)[1]
-                st_d(q, 0)
-                st_d(q, 1)
-            for r, q in squashes(t + 1):
-                st_a3(q)
-                st_a4(q)
+                st_b(t, 0)
+            if sq1:
+                st_a4(*sq1, xe[t - 1])
+            weigh(1)
+            if e is not None:
+                st_e2(e)
+                st_e3(e)
+            if is_unit(t):
+                st_b(t, 1)
             proj_step()
             if is_unit(t - 1):
-                q = unit(t - 1)[1]
-                st_c(q, 0)
-                st_c(q, 1)
+                st_c((t - 1) % NG, 0)
+                st_c((t - 1) % NG, 1)
             if is_unit(t - 3):
-                q = unit(t - 3)[1]
-                st_f(q, 0)
-                st_f(q, 1)
-            if is_unit(t - 4):
-                st_g(unit(t - 4)[1], 0)
-            if is_unit(t - 2):
-                q = unit(t - 2)[1]
-                st_e1(q)
-                st_e2(q)
+                st_f((t - 3) % NG, 0)
+                st_f((t - 3) % NG, 1)
+            weigh(2)
+            if e is not None:
+                st_e4(e)
+            weigh(3)
+            if e is not None:
+                st_e5(e)
             proj_step()
-            if is_unit(t - 4):
-                st_g(unit(t - 4)[1], 1)
-            if is_unit(t - 2):
-                q = unit(t - 2)[1]
-                st_e3(q)
-                st_e4(q, 0)
-                st_e4(q, 1)
-            if is_unit(t - 4):
-                st_go3(unit(t - 4)[1])
-            for r, q in squashes(t + 1):
-                st_a5(q, r)
-            for r, q in squashes(t + 2):
-                st_a2(q)
+            weigh(4)
+            if e is not None:
+                st_e6(e)
+                st_e7(e, 0)
+                st_e7(e, 1)
+            weigh(5, 6, 7)
+            if g is not None:
+                st_go3(g)
+            if sq:
+                xe[t] = st_a2(sq[0], ssq)
 
         of_ps = psum_y.tile([P, P], F32, name="of_ps", tag="Y")
         nc.tensor.transpose(of_ps[:], ofin[:], ident[:])

@@ -29,7 +29,7 @@ PIN = True
 
 
 def gpsimd_scales(k, i):
-    return i not in (0, 1, 4)
+    return i not in ((0, 1, 4) if k % 2 == 0 else (0, 1, 4, 5))
 
 
 def gpsimd_sums(k):
@@ -52,7 +52,7 @@ def tile_capsule_t_kernel(tc, inputs, W, out):
         qpool = ctx.enter_context(tc.tile_pool(name="qpool", bufs=2))
         upool = ctx.enter_context(tc.tile_pool(name="upool", bufs=NG))
         wpool = ctx.enter_context(tc.tile_pool(name="wpool", bufs=4))
-        cpool = ctx.enter_context(tc.tile_pool(name="cpool", bufs=3))
+        cpool = ctx.enter_context(tc.tile_pool(name="cpool", bufs=4))
         opool = ctx.enter_context(tc.tile_pool(name="opool", bufs=2))
         small = ctx.enter_context(tc.tile_pool(name="small", bufs=NG + 1))
         psum_n = ctx.enter_context(tc.psum_pool(name="psum_n", bufs=1))
@@ -71,8 +71,9 @@ def tile_capsule_t_kernel(tc, inputs, W, out):
         nc.vector.tensor_copy(out=blk[:], in_=m8[:].unsqueeze(2).to_broadcast([P, NCAP, DL]))
         neghalf = const.tile([P, 2 * GB], F32, name="neghalf")
         nc.vector.memset(neghalf[:], -0.5)
-        epsc = const.tile([P, 1], F32, name="epsc")
-        nc.vector.memset(epsc[:], EPS)
+        epsc = const.tile([P, 2], F32, name="epsc")
+        nc.vector.memset(epsc[:, 0:1], EPS)
+        nc.vector.memset(epsc[:, 1:2], NCAP * NCAP * EPS)
         ofin = const.tile([P, P], F32, name="ofin")
         nc.vector.memset(ofin[:], 0.0)
         junk = const.tile([P, S], F32, name="junk")
@@ -188,16 +189,14 @@ def tile_capsule_t_kernel(tc, inputs, W, out):
                     )
 
         def st_a1(qs, r):
-            pre = 1.0 / NCAP if r == 0 else 1.0
-            sqj = small.tile([P, DH], F32, name="sqj")
             ssq = small.tile([P, 2 * GB], F32, name="ssq")
             for i, q in enumerate(qs):
                 for bl in range(GB):
+                    sqj = small.tile([P, DH], F32, name="sqj")
                     nc.scalar.activation(
                         out=sqj[:],
                         in_=st[q]["v"][:, bl, :],
                         func=ACT.Square,
-                        scale=pre,
                         accum_out=ssq[:, i * GB + bl : i * GB + bl + 1],
                     )
             return ssq
@@ -212,39 +211,45 @@ def tile_capsule_t_kernel(tc, inputs, W, out):
                 start=True,
                 stop=True,
             )
+            return n_ps
+
+        def st_a3(qs, r, n_ps):
+            n = len(qs) * GB
             xe = small.tile([P, 2 * GB], F32, name="xe")
             nc.scalar.activation(
-                out=xe[:, 0:n], in_=n_ps[:, 0:n], func=ACT.Identity, bias=epsc[:, 0:1]
+                out=xe[:, 0:n],
+                in_=n_ps[:, 0:n],
+                func=ACT.Identity,
+                bias=epsc[:, 0:1] if r > 0 else epsc[:, 1:2],
             )
-            return xe
-
-        def st_a4(qs, r, xe):
-            n = len(qs) * GB
             rs = small.tile([P, 2 * GB], F32, name="rs")
             nc.gpsimd.tensor_tensor(out=rs[:, 0:n], in0=xe[:, 0:n], in1=neghalf[:, 0:n], op=ALU.pow)
+            return rs
+
+        def st_a4(qs, r, rs):
             for i, q in enumerate(qs):
                 s = st[q]
-                rsb = rs[:, i * GB : (i + 1) * GB].unsqueeze(2).to_broadcast([P, GB, DH])
-                if r == ROUNDS - 1:
-                    nc.gpsimd.tensor_tensor(
-                        out=ofin[:, 0 : DH * B].rearrange("p (dh b) -> p b dh", dh=DH)[
-                            :, q * GB : (q + 1) * GB, :
-                        ],
-                        in0=s["v"][:],
-                        in1=rsb,
-                        op=ALU.mult,
-                    )
-                    continue
-                o = small.tile([P, GB, DH], F32, name="o")
-                nc.gpsimd.tensor_tensor(out=o[:], in0=s["v"][:], in1=rsb, op=ALU.mult)
                 if r == 0:
-                    ocum = small.tile([P, GB, DH], F32, name="ocum")
-                    nc.gpsimd.tensor_scalar(
-                        out=ocum[:], in0=o[:], scalar1=1.0 / NCAP, scalar2=0.0, op0=ALU.mult, op1=ALU.add
-                    )
-                    s["ocum"] = ocum
+                    s["ocum"] = small.tile([P, GB, DH], F32, name="ocum")
+                    o = s["ocum"][:]
+                elif r < ROUNDS - 1:
+                    s["o"] = small.tile([P, GB, DH], F32, name="o")
+                    o = s["o"][:]
                 else:
-                    nc.gpsimd.tensor_tensor(out=s["ocum"][:], in0=s["ocum"][:], in1=o[:], op=ALU.add)
+                    o = ofin[:, 0 : DH * B].rearrange("p (dh b) -> p b dh", dh=DH)[:, q * GB : (q + 1) * GB, :]
+                for bl in range(GB):
+                    nc.scalar.activation(
+                        out=o[:, bl, :],
+                        in_=s["v"][:, bl, :],
+                        func=ACT.Copy,
+                        scale=rs[:, i * GB + bl : i * GB + bl + 1],
+                    )
+
+        def st_a5(qs, r):
+            if 0 < r < ROUNDS - 1:
+                for q in qs:
+                    s = st[q]
+                    nc.gpsimd.tensor_tensor(out=s["ocum"][:], in0=s["ocum"][:], in1=s["o"][:], op=ALU.add)
 
         def st_b(k, bl):
             s = st[k % NG]
@@ -296,25 +301,19 @@ def tile_capsule_t_kernel(tc, inputs, W, out):
 
         def st_e1(q):
             s = st[q]
-            mx = small.tile([P, A], F32, name="mx")
-            nc.vector.tensor_reduce(out=mx[:], in_=s["t"][:], axis=AX.X, op=ALU.max)
-            s["mx"] = mx
+            nmx = small.tile([P, A], F32, name="nmx")
+            nc.vector.tensor_reduce(
+                out=nmx[:], in_=s["t"][:], axis=AX.X, op=ALU.max, negate=True
+            )
+            s["nmx"] = nmx
 
         def st_e2(q):
             s = st[q]
-            td = small.tile([P, A, NCAP], F32, name="td")
-            nc.vector.tensor_tensor(
-                out=td[:],
-                in0=s["t"][:],
-                in1=s["mx"][:].unsqueeze(2).to_broadcast([P, A, NCAP]),
-                op=ALU.subtract,
-            )
-            s["td"] = td
-
-        def st_e3(q):
-            s = st[q]
             ex = small.tile([P, A, NCAP], F32, name="ex")
-            nc.scalar.activation(out=ex[:], in_=s["td"][:], func=ACT.Exp)
+            for a in range(A):
+                nc.scalar.activation(
+                    out=ex[:, a, :], in_=s["t"][:, a, :], func=ACT.Exp, bias=s["nmx"][:, a : a + 1]
+                )
             s["ex"] = ex
 
         def st_e4(q):
@@ -329,27 +328,17 @@ def tile_capsule_t_kernel(tc, inputs, W, out):
             nc.vector.reciprocal(out=rc[:], in_=s["sm"][:])
             s["rc"] = rc
 
-        def st_e6(q):
-            s = st[q]
-            c = small.tile([P, A, NCAP], F32, name="c")
-            nc.vector.tensor_tensor(
-                out=c[:],
-                in0=s["ex"][:],
-                in1=s["rc"][:].unsqueeze(2).to_broadcast([P, A, NCAP]),
-                op=ALU.mult,
-            )
-            s["c"] = c
-
         def st_e7(q, bl):
             s = st[q]
-            crep = cpool.tile([P, SJ * NCAP, DL], F32, name="crep")
-            nc.scalar.copy(
-                out=crep[:],
-                in_=s["c"][:, bl * SJ : (bl + 1) * SJ, :]
-                .rearrange("p j n -> p (j n)")
-                .unsqueeze(2)
-                .to_broadcast([P, SJ * NCAP, DL]),
-            )
+            crep = cpool.tile([P, SJ, NCAP, DL], F32, name="crep")
+            for j in range(SJ):
+                a = bl * SJ + j
+                nc.scalar.activation(
+                    out=crep[:, j],
+                    in_=s["ex"][:, a, :].unsqueeze(2).to_broadcast([P, NCAP, DL]),
+                    func=ACT.Copy,
+                    scale=s["rc"][:, a : a + 1],
+                )
             s["crep", bl] = crep
 
         def st_f(q, bl):
@@ -358,7 +347,7 @@ def tile_capsule_t_kernel(tc, inputs, W, out):
             for j in range(SJ):
                 nc.tensor.transpose(
                     cb[:, j, :],
-                    s["crep", bl][:, j * NCAP : (j + 1) * NCAP, :].rearrange("p n dl -> p (n dl)"),
+                    s["crep", bl][:, j].rearrange("p n dl -> p (n dl)"),
                     ident[:],
                 )
             s["cb", bl] = cb
@@ -443,7 +432,7 @@ def tile_capsule_t_kernel(tc, inputs, W, out):
         while step[0] < LEAD:
             proj_step()
 
-        xe = {}
+        n_ps = {}
         for t in range(-2, NU + SQUASH_LAG):
             g = t - 4 if is_unit(t - 4) else None
             e = (t - 2) % NG if is_unit(t - 2) else None
@@ -469,13 +458,14 @@ def tile_capsule_t_kernel(tc, inputs, W, out):
             if is_unit(t):
                 st_b(t, 0)
             if sq1:
-                st_a4(*sq1, xe[t - 1])
+                rs = st_a3(*sq1, n_ps[t - 1])
             weigh(1)
             if e is not None:
                 st_e2(e)
-                st_e3(e)
             if is_unit(t):
                 st_b(t, 1)
+            if g is not None:
+                st_go3(g)
             proj_step()
             if is_unit(t - 1):
                 st_c((t - 1) % NG, 0)
@@ -483,23 +473,22 @@ def tile_capsule_t_kernel(tc, inputs, W, out):
             if is_unit(t - 3):
                 st_f((t - 3) % NG, 0)
                 st_f((t - 3) % NG, 1)
-            weigh(2)
+            if sq1:
+                st_a4(*sq1, rs)
+                st_a5(*sq1)
+            weigh(2, 3)
             if e is not None:
                 st_e4(e)
-            weigh(3)
+            weigh(4)
             if e is not None:
                 st_e5(e)
             proj_step()
-            weigh(4)
             if e is not None:
-                st_e6(e)
                 st_e7(e, 0)
                 st_e7(e, 1)
             weigh(5, 6, 7)
-            if g is not None:
-                st_go3(g)
             if sq:
-                xe[t] = st_a2(sq[0], ssq)
+                n_ps[t] = st_a2(sq[0], ssq)
 
         of_ps = psum_y.tile([P, P], F32, name="of_ps", tag="Y")
         nc.tensor.transpose(of_ps[:], ofin[:], ident[:])

@@ -53,6 +53,7 @@ def tile_capsule_t_kernel(tc, inputs, W, out):
         upool = ctx.enter_context(tc.tile_pool(name="upool", bufs=NG))
         wpool = ctx.enter_context(tc.tile_pool(name="wpool", bufs=4))
         cpool = ctx.enter_context(tc.tile_pool(name="cpool", bufs=4))
+        jpool = ctx.enter_context(tc.tile_pool(name="jpool", bufs=4))
         opool = ctx.enter_context(tc.tile_pool(name="opool", bufs=2))
         small = ctx.enter_context(tc.tile_pool(name="small", bufs=NG + 1))
         psum_n = ctx.enter_context(tc.psum_pool(name="psum_n", bufs=1))
@@ -76,7 +77,6 @@ def tile_capsule_t_kernel(tc, inputs, W, out):
         nc.vector.memset(epsc[:, 1:2], NCAP * NCAP * EPS)
         ofin = const.tile([P, P], F32, name="ofin")
         nc.vector.memset(ofin[:], 0.0)
-        junk = const.tile([P, S], F32, name="junk")
         junk_s = const.tile([P, S], F32, name="junk_s")
 
         xin = inputs.rearrange("(j p) b h -> p j b h", p=P)
@@ -356,8 +356,9 @@ def tile_capsule_t_kernel(tc, inputs, W, out):
             s = st[k % NG]
             if i == 0:
                 s["v"] = small.tile([P, GB, DH], F32, name="v")
+            products = jpool.tile([P, S], F32, name="products")
             nc.vector.scalar_tensor_tensor(
-                out=junk[:],
+                out=products[:],
                 in0=s["u"][:, i // DH, i % DH, :],
                 scalar=1.0,
                 in1=s["cb", i // DH][:].rearrange("p j s -> p (j s)"),
@@ -473,9 +474,6 @@ def tile_capsule_t_kernel(tc, inputs, W, out):
             if is_unit(t - 3):
                 st_f((t - 3) % NG, 0)
                 st_f((t - 3) % NG, 1)
-            if sq1:
-                st_a4(*sq1, rs)
-                st_a5(*sq1)
             weigh(2, 3)
             if e is not None:
                 st_e4(e)
@@ -486,6 +484,9 @@ def tile_capsule_t_kernel(tc, inputs, W, out):
             if e is not None:
                 st_e7(e, 0)
                 st_e7(e, 1)
+            if sq1:
+                st_a4(*sq1, rs)
+                st_a5(*sq1)
             weigh(5, 6, 7)
             if sq:
                 n_ps[t] = st_a2(sq[0], ssq)

@@ -84,23 +84,27 @@ def tile_capsule_t_kernel(tc, inputs, W, out):
         for q in range(NG):
             st[q] = {}
 
-        def load(q):
-            x = xpool.tile([P, SJ, GB, H], BF16, name="x")
-            nc.sync.dma_start(out=x[:], in_=xin[:, :, q * GB : (q + 1) * GB, :])
-            st[q]["x32"] = x[:].bitcast(F32)
+        def load(q, bl):
+            if bl == 0:
+                x = xpool.tile([P, GB, SJ, H], BF16, name="x")
+                st[q]["x"] = x
+            nc.sync.dma_start(out=st[q]["x"][:, bl], in_=xin[:, :, q * GB + bl, :])
 
-        load(0)
+        load(0, 0)
         wraw = const.tile([P, 4, NCAP * DC], BF16, name="wraw")
         nc.sync.dma_start(
             out=wraw[:],
             in_=W[0].rearrange("(p t) c -> p t c", t=4),
         )
-        load(1)
+        load(0, 1)
+        load(1, 0)
+        load(1, 1)
         loaded = [2]
 
         def load_up_to(n):
             while loaded[0] < min(n, NG):
-                load(loaded[0])
+                load(loaded[0], 0)
+                load(loaded[0], 1)
                 loaded[0] += 1
 
         wg = const.tile([P, DH, NCAP, DL, 4], BF16, name="wg", align_bytes=64)
@@ -124,7 +128,7 @@ def tile_capsule_t_kernel(tc, inputs, W, out):
                     for uu in range(2):
                         nc.tensor.transpose(
                             xt[:, jj, uu, :],
-                            s["x32"][:, 2 * half + jj, bl, uu : 2 * P : 2],
+                            s["x"][:].bitcast(F32)[:, bl, 2 * half + jj, uu : 2 * P : 2],
                             ident[:],
                         )
                 tiles.append(xt)
@@ -408,8 +412,10 @@ def tile_capsule_t_kernel(tc, inputs, W, out):
             if NG <= k < NU and k % 2 == 0:
                 return ([k % NG, k % NG + 1], k // NG)
             q = t - (NU - NG) - SQUASH_LAG
-            if 0 <= q < NG and q % 2 == 0:
+            if 0 <= q < NG - 2 and q % 2 == 0:
                 return ([q, q + 1], ROUNDS - 1)
+            if NG - 3 <= q < NG - 1:
+                return ([q + 1], ROUNDS - 1)
             return None
 
         def is_batch(b):

@@ -24,23 +24,23 @@ A = GB * SJ
 EPS = 1e-7
 NU = (ROUNDS - 1) * NG
 SQUASH_LAG = 6
-LEAD = 8
+LEAD = 4
 PIN = True
 
 
 def gpsimd_scales(k, i):
-    return i not in ((0, 1, 4) if k % 2 == 0 else (0, 1, 4, 5))
+    return i != 0 if k < 4 else i not in ((0, 1, 4, 5) if k % 2 == 0 else (0, 1, 2, 4, 5))
 
 
 def gpsimd_sums(k):
-    return 1
+    return 2 if k % 4 == 0 else 1
 
 
 FLOPS = 2 * S * B * H * NCAP * DC + (2 * ROUNDS - 1) * 2 * S * B * NCAP * DC
 
 
 def vector_evac_dh(b):
-    return (1, 3)
+    return (0, 1, 3) if b % 2 else (1, 3)
 
 
 def tile_capsule_t_kernel(tc, inputs, W, out):
@@ -474,12 +474,6 @@ def tile_capsule_t_kernel(tc, inputs, W, out):
             if g is not None:
                 st_go3(g)
             proj_step()
-            if is_unit(t - 1):
-                st_c((t - 1) % NG, 0)
-                st_c((t - 1) % NG, 1)
-            if is_unit(t - 3):
-                st_f((t - 3) % NG, 0)
-                st_f((t - 3) % NG, 1)
             weigh(2, 3)
             if e is not None:
                 st_e4(e)
@@ -487,6 +481,12 @@ def tile_capsule_t_kernel(tc, inputs, W, out):
             if e is not None:
                 st_e5(e)
             proj_step()
+            if is_unit(t - 1):
+                st_c((t - 1) % NG, 0)
+                st_c((t - 1) % NG, 1)
+            if is_unit(t - 3):
+                st_f((t - 3) % NG, 0)
+                st_f((t - 3) % NG, 1)
             if e is not None:
                 st_e7(e, 0)
                 st_e7(e, 1)

from contextlib import ExitStack

import concourse.masks as masks
import concourse.mybir as mybir

F32 = mybir.dt.float32
BF16 = mybir.dt.bfloat16
U32 = mybir.dt.uint32
U8 = mybir.dt.uint8
FP8X4 = mybir.dt.float8_e4m3fn_x4
ALU = mybir.AluOpType
ACT = mybir.ActivationFunctionType
AX = mybir.AxisListType

S, B, H, NCAP, DC = 512, 16, 512, 8, 64
ROUNDS = 4
P = 128
SJ = S // P
DH = 4
DL = DC // DH
GB = 2
NG = B // GB
A = GB * SJ
EPS = 1e-7
NU = (ROUNDS - 1) * NG
SQUASH_LAG = 6
LEAD = 4
PIN = True


def gpsimd_scales(k, i):
    return i != 0 if k < 4 else i not in ((0, 1, 4, 5) if k % 2 == 0 else (0, 1, 2, 4, 5))


def gpsimd_sums(k):
    return 2 if k % 4 == 0 else 1


FLOPS = 2 * S * B * H * NCAP * DC + (2 * ROUNDS - 1) * 2 * S * B * NCAP * DC


def vector_evac_dh(b):
    return (0, 1, 3) if b % 2 else (1, 3)


def tile_capsule_t_kernel(tc, inputs, W, out):
    nc = tc.nc
    with ExitStack() as ctx:
        const = ctx.enter_context(tc.tile_pool(name="const", bufs=1))
        xpool = ctx.enter_context(tc.tile_pool(name="xpool", bufs=2))
        gpool = ctx.enter_context(tc.tile_pool(name="gpool", bufs=2))
        qpool = ctx.enter_context(tc.tile_pool(name="qpool", bufs=2))
        upool = ctx.enter_context(tc.tile_pool(name="upool", bufs=NG))
        wpool = ctx.enter_context(tc.tile_pool(name="wpool", bufs=4))
        cpool = ctx.enter_context(tc.tile_pool(name="cpool", bufs=4))
        jpool = ctx.enter_context(tc.tile_pool(name="jpool", bufs=4))
        opool = ctx.enter_context(tc.tile_pool(name="opool", bufs=2))
        small = ctx.enter_context(tc.tile_pool(name="small", bufs=NG + 1))
        psum_n = ctx.enter_context(tc.psum_pool(name="psum_n", bufs=1))
        psum_x = ctx.enter_context(tc.psum_pool(name="psum_x", bufs=4))
        psum_y = ctx.enter_context(tc.psum_pool(name="psum_y", bufs=3))
        if PIN:
            ctx.enter_context(tc.manual_schedule())

        ident = const.tile([P, P], F32, name="ident")
        masks.make_identity(nc, ident[:])
        m8 = const.tile([P, NCAP], F32, name="m8")
        nc.vector.tensor_reduce(
            out=m8[:], in_=ident[:].rearrange("p (n dl) -> p n dl", dl=DL), axis=AX.X, op=ALU.add
        )
        blk = const.tile([P, NCAP, DL], F32, name="blk")
        nc.vector.tensor_copy(out=blk[:], in_=m8[:].unsqueeze(2).to_broadcast([P, NCAP, DL]))
        neghalf = const.tile([P, 2 * GB], F32, name="neghalf")
        nc.vector.memset(neghalf[:], -0.5)
        epsc = const.tile([P, 2], F32, name="epsc")
        nc.vector.memset(epsc[:, 0:1], EPS)
        nc.vector.memset(epsc[:, 1:2], NCAP * NCAP * EPS)
        ofin = const.tile([P, P], F32, name="ofin")
        nc.vector.memset(ofin[:], 0.0)
        junk_s = const.tile([P, S], F32, name="junk_s")

        xin = inputs.rearrange("(j p) b h -> p j b h", p=P)
        st = {}
        for q in range(NG):
            st[q] = {}

        def load(q, bl):
            if bl == 0:
                x = xpool.tile([P, GB, SJ, H], BF16, name="x")
                st[q]["x"] = x
            nc.sync.dma_start(out=st[q]["x"][:, bl], in_=xin[:, :, q * GB + bl, :])

        load(0, 0)
        wraw = const.tile([P, 4, NCAP * DC], BF16, name="wraw")
        nc.sync.dma_start(
            out=wraw[:],
            in_=W[0].rearrange("(p t) c -> p t c", t=4),
        )
        load(0, 1)
        load(1, 0)
        load(1, 1)
        loaded = [2]

        def load_up_to(n):
            while loaded[0] < min(n, NG):
                load(loaded[0], 0)
                load(loaded[0], 1)
                loaded[0] += 1

        wg = const.tile([P, DH, NCAP, DL, 4], BF16, name="wg", align_bytes=64)
        wview = wraw[:].rearrange("p t (n dh dl) -> p dh n dl t", dh=DH, dl=DL)
        for dh in range(DH):
            nc.vector.tensor_copy(out=wg[:, dh], in_=wview[:, dh])
        wq = const.tile([P, NCAP * DC], U32, name="wq", align_bytes=64)
        ws = const.tile([P, NCAP * DC], U8, name="ws", align_bytes=64)
        nc.vector.quantize_mx(
            out=wq[:].bitcast(FP8X4),
            scales=ws[:],
            in_=wg[:].rearrange("p dh n dl t -> p (dh n dl t)"),
        )

        def st_t(q, bl):
            s = st[q]
            tiles = []
            for half in range(2):
                xt = psum_y.tile([P, 2, 2, P], F32, name="xt", tag="Y")
                for jj in range(2):
                    for uu in range(2):
                        nc.tensor.transpose(
                            xt[:, jj, uu, :],
                            s["x"][:].bitcast(F32)[:, bl, 2 * half + jj, uu : 2 * P : 2],
                            ident[:],
                        )
                tiles.append(xt)
            s["xt", bl] = tiles

        def st_xc(q, bl):
            s = st[q]
            grouped = gpool.tile([P, 4 * S], BF16, name="grouped", align_bytes=64)
            g32 = grouped[:].bitcast(F32)
            for half in range(2):
                nc.scalar.copy(
                    out=g32[:, 512 * half : 512 * half + 512].rearrange(
                        "p (jj s uu) -> p jj s uu", jj=2, uu=2
                    ),
                    in_=s["xt", bl][half][:].rearrange("p jj uu s -> p jj s uu"),
                )
            s["grouped", bl] = grouped

        def st_q(q, bl):
            s = st[q]
            xq = qpool.tile([P, S], U32, name="xq", align_bytes=64)
            xs = qpool.tile([P, S], U8, name="xs", align_bytes=64)
            nc.vector.quantize_mx(
                out=xq[:].bitcast(FP8X4), scales=xs[:], in_=s["grouped", bl][:]
            )
            s["xq", bl] = (xq, xs)

        def st_mev(q, bl):
            s = st[q]
            xq, xs = s["xq", bl]
            if bl == 0:
                s["u"] = upool.tile([P, GB, DH, S], F32, name="u")
                s["v"] = small.tile([P, GB, DH], F32, name="v")
            for dh in range(DH):
                pb = psum_x.tile([P, S], F32, name="pb", tag="X")
                nc.tensor.matmul_mx(
                    out=pb[:],
                    lhsT=wq[:, P * dh : P * dh + P].bitcast(FP8X4),
                    lhsT_scale=ws[:, P * dh : P * dh + P],
                    rhs=xq[:].bitcast(FP8X4),
                    rhs_scale=xs[:],
                    start=True,
                    stop=True,
                )
                s["pb", bl, dh] = pb
                if dh in vector_evac_dh(q * GB + bl):
                    nc.vector.tensor_scalar(
                        out=s["u"][:, bl, dh, :],
                        in0=s["pb", bl, dh][:],
                        scalar1=1.0,
                        scalar2=None,
                        op0=ALU.mult,
                        op1=ALU.add,
                        accum_out=s["v"][:, bl, dh : dh + 1],
                    )
                else:
                    nc.scalar.activation(
                        out=s["u"][:, bl, dh, :],
                        in_=s["pb", bl, dh][:],
                        func=ACT.Copy,
                        accum_out=s["v"][:, bl, dh : dh + 1],
                    )

        def st_a1(qs, r):
            ssq = small.tile([P, 2 * GB], F32, name="ssq")
            for i, q in enumerate(qs):
                for bl in range(GB):
                    sqj = small.tile([P, DH], F32, name="sqj")
                    nc.scalar.activation(
                        out=sqj[:],
                        in_=st[q]["v"][:, bl, :],
                        func=ACT.Square,
                        accum_out=ssq[:, i * GB + bl : i * GB + bl + 1],
                    )
            return ssq

        def st_a2(qs, ssq):
            n = len(qs) * GB
            n_ps = psum_n.tile([P, 2 * GB], F32, name="n_ps", tag="n")
            nc.tensor.matmul(
                out=n_ps[:, 0:n],
                lhsT=blk[:].rearrange("p n dl -> p (n dl)"),
                rhs=ssq[:, 0:n],
                start=True,
                stop=True,
            )
            return n_ps

        def st_a3(qs, r, n_ps):
            n = len(qs) * GB
            xe = small.tile([P, 2 * GB], F32, name="xe")
            nc.scalar.activation(
                out=xe[:, 0:n],
                in_=n_ps[:, 0:n],
                func=ACT.Identity,
                bias=epsc[:, 0:1] if r > 0 else epsc[:, 1:2],
            )
            rs = small.tile([P, 2 * GB], F32, name="rs")
            nc.gpsimd.tensor_tensor(out=rs[:, 0:n], in0=xe[:, 0:n], in1=neghalf[:, 0:n], op=ALU.pow)
            return rs

        def st_a4(qs, r, rs):
            for i, q in enumerate(qs):
                s = st[q]
                if r == 0:
                    s["ocum"] = small.tile([P, GB, DH], F32, name="ocum")
                    o = s["ocum"][:]
                elif r < ROUNDS - 1:
                    s["o"] = small.tile([P, GB, DH], F32, name="o")
                    o = s["o"][:]
                else:
                    o = ofin[:, 0 : DH * B].rearrange("p (dh b) -> p b dh", dh=DH)[:, q * GB : (q + 1) * GB, :]
                for bl in range(GB):
                    nc.scalar.activation(
                        out=o[:, bl, :],
                        in_=s["v"][:, bl, :],
                        func=ACT.Copy,
                        scale=rs[:, i * GB + bl : i * GB + bl + 1],
                    )

        def st_a5(qs, r):
            if 0 < r < ROUNDS - 1:
                for q in qs:
                    s = st[q]
                    nc.gpsimd.tensor_tensor(out=s["ocum"][:], in0=s["ocum"][:], in1=s["o"][:], op=ALU.add)

        def st_b(k, bl):
            s = st[k % NG]
            wt = wpool.tile([P, DH, S], F32, name="wt")
            for dh in range(DH):
                if gpsimd_scales(k, bl * DH + dh):
                    nc.gpsimd.tensor_scalar(
                        out=wt[:, dh, :],
                        in0=s["u"][:, bl, dh, :],
                        scalar1=s["ocum"][:, bl, dh : dh + 1],
                        scalar2=0.0,
                        op0=ALU.mult,
                        op1=ALU.add,
                    )
                else:
                    nc.scalar.activation(
                        out=wt[:, dh, :],
                        in_=s["u"][:, bl, dh, :],
                        func=ACT.Copy,
                        scale=s["ocum"][:, bl, dh : dh + 1],
                    )
            s["wt", bl] = wt

        def st_c(q, bl):
            s = st[q]
            tp = psum_y.tile([P, SJ, P], F32, name="tp", tag="Y")
            for j in range(SJ):
                for dh in range(DH):
                    nc.tensor.matmul(
                        out=tp[:, j, :],
                        lhsT=s["wt", bl][:, dh, P * j : P * j + P],
                        rhs=ident[:],
                        is_transpose=True,
                        start=(dh == 0),
                        stop=(dh == DH - 1),
                    )
            s["tp", bl] = tp

        def st_d(q, bl):
            s = st[q]
            if bl == 0:
                s["t"] = small.tile([P, A, NCAP], F32, name="t")
            nc.vector.tensor_reduce(
                out=s["t"][:, bl * SJ : (bl + 1) * SJ, :],
                in_=s["tp", bl][:].rearrange("p j (n dl) -> p j n dl", dl=DL),
                axis=AX.X,
                op=ALU.add,
            )

        def st_e1(q):
            s = st[q]
            nmx = small.tile([P, A], F32, name="nmx")
            nc.vector.tensor_reduce(
                out=nmx[:], in_=s["t"][:], axis=AX.X, op=ALU.max, negate=True
            )
            s["nmx"] = nmx

        def st_e2(q):
            s = st[q]
            ex = small.tile([P, A, NCAP], F32, name="ex")
            for a in range(A):
                nc.scalar.activation(
                    out=ex[:, a, :], in_=s["t"][:, a, :], func=ACT.Exp, bias=s["nmx"][:, a : a + 1]
                )
            s["ex"] = ex

        def st_e4(q):
            s = st[q]
            sm = small.tile([P, A], F32, name="sm")
            nc.vector.tensor_reduce(out=sm[:], in_=s["ex"][:], axis=AX.X, op=ALU.add)
            s["sm"] = sm

        def st_e5(q):
            s = st[q]
            rc = small.tile([P, A], F32, name="rc")
            nc.vector.reciprocal(out=rc[:], in_=s["sm"][:])
            s["rc"] = rc

        def st_e7(q, bl):
            s = st[q]
            crep = cpool.tile([P, SJ, NCAP, DL], F32, name="crep")
            for j in range(SJ):
                a = bl * SJ + j
                nc.scalar.activation(
                    out=crep[:, j],
                    in_=s["ex"][:, a, :].unsqueeze(2).to_broadcast([P, NCAP, DL]),
                    func=ACT.Copy,
                    scale=s["rc"][:, a : a + 1],
                )
            s["crep", bl] = crep

        def st_f(q, bl):
            s = st[q]
            cb = psum_x.tile([P, SJ, P], F32, name="cb", tag="X")
            for j in range(SJ):
                nc.tensor.transpose(
                    cb[:, j, :],
                    s["crep", bl][:, j].rearrange("p n dl -> p (n dl)"),
                    ident[:],
                )
            s["cb", bl] = cb

        def st_g(k, i):
            s = st[k % NG]
            if i == 0:
                s["v"] = small.tile([P, GB, DH], F32, name="v")
            products = jpool.tile([P, S], F32, name="products")
            nc.vector.scalar_tensor_tensor(
                out=products[:],
                in0=s["u"][:, i // DH, i % DH, :],
                scalar=1.0,
                in1=s["cb", i // DH][:].rearrange("p j s -> p (j s)"),
                op0=ALU.mult,
                op1=ALU.mult,
                accum_out=s["v"][:, i // DH, i % DH : i % DH + 1],
            )

        def st_go1(k):
            n = gpsimd_sums(k)
            if n == 0:
                return
            s = st[k % NG]
            cbs = opool.tile([P, S], F32, name="cbs")
            nc.scalar.copy(out=cbs[:], in_=s["cb", 1][:].rearrange("p j s -> p (j s)"))
            prod = opool.tile([P, n, S], F32, name="prod")
            nc.gpsimd.tensor_tensor(
                out=prod[:],
                in0=s["u"][:, 1, DH - n :, :],
                in1=cbs[:].unsqueeze(1).to_broadcast([P, n, S]),
                op=ALU.mult,
            )
            s["prod"] = prod

        def st_go3(k):
            n = gpsimd_sums(k)
            s = st[k % NG]
            for i in range(n):
                dh = DH - n + i
                nc.scalar.activation(
                    out=junk_s[:],
                    in_=s["prod"][:, i, :],
                    func=ACT.Copy,
                    accum_out=s["v"][:, 1, dh : dh + 1],
                )

        def unit(k):
            return (k // NG, k % NG)

        def is_unit(k):
            return 0 <= k < NU

        def squash_of(t):
            k = t + 2
            if 0 <= k < NG:
                return ([k], 0)
            if NG <= k < NU and k % 2 == 0:
                return ([k % NG, k % NG + 1], k // NG)
            q = t - (NU - NG) - SQUASH_LAG
            if 0 <= q < NG - 2 and q % 2 == 0:
                return ([q, q + 1], ROUNDS - 1)
            if NG - 3 <= q < NG - 1:
                return ([q + 1], ROUNDS - 1)
            return None

        def is_batch(b):
            return 0 <= b < B

        step = [-2]

        def proj_step():
            b = step[0]
            step[0] += 1
            if is_batch(b + 2) and (b + 2) % GB == 0:
                load_up_to((b + 2) // GB + 2)
            if is_batch(b + 1):
                st_q((b + 1) // GB, (b + 1) % GB)
            if is_batch(b):
                st_mev(b // GB, b % GB)
            if is_batch(b + 2):
                st_t((b + 2) // GB, (b + 2) % GB)
                st_xc((b + 2) // GB, (b + 2) % GB)

        while step[0] < LEAD:
            proj_step()

        n_ps = {}
        for t in range(-2, NU + SQUASH_LAG):
            g = t - 4 if is_unit(t - 4) else None
            e = (t - 2) % NG if is_unit(t - 2) else None
            sq = squash_of(t)
            sq1 = squash_of(t - 1)

            def weigh(*todo):
                if g is not None:
                    for i in todo:
                        if i < GB * DH - gpsimd_sums(g):
                            st_g(g, i)

            if sq:
                ssq = st_a1(*sq)
            if g is not None:
                st_go1(g)
            if e is not None:
                st_d(e, 0)
                st_d(e, 1)
            weigh(0)
            if e is not None:
                st_e1(e)
            if is_unit(t):
                st_b(t, 0)
            if sq1:
                rs = st_a3(*sq1, n_ps[t - 1])
            weigh(1)
            if e is not None:
                st_e2(e)
            if is_unit(t):
                st_b(t, 1)
            if g is not None:
                st_go3(g)
            proj_step()
            weigh(2, 3)
            if e is not None:
                st_e4(e)
            weigh(4)
            if e is not None:
                st_e5(e)
            proj_step()
            if is_unit(t - 1):
                st_c((t - 1) % NG, 0)
                st_c((t - 1) % NG, 1)
            if is_unit(t - 3):
                st_f((t - 3) % NG, 0)
                st_f((t - 3) % NG, 1)
            if e is not None:
                st_e7(e, 0)
                st_e7(e, 1)
            if sq1:
                st_a4(*sq1, rs)
                st_a5(*sq1)
            weigh(5, 6, 7)
            if sq:
                n_ps[t] = st_a2(sq[0], ssq)

        of_ps = psum_y.tile([P, P], F32, name="of_ps", tag="Y")
        nc.tensor.transpose(of_ps[:], ofin[:], ident[:])
        of_sb = const.tile([P, NCAP, DL], F32, name="of_sb")
        nc.vector.tensor_copy(out=of_sb[:].rearrange("p n dl -> p (n dl)"), in_=of_ps[:])
        for dh in range(DH):
            nc.sync.dma_start(
                out=out[:, :, DL * dh : DL * dh + DL], in_=of_sb[B * dh : B * dh + B, :, :]
            )
